import numpy as np
import ml_dtypes


def mxq(x, axis, fmt="e4m3"):
    dtype, down = {"e4m3": (ml_dtypes.float8_e4m3fn, 7), "e5m2": (ml_dtypes.float8_e5m2, 14)}[fmt]
    v = np.moveaxis(np.asarray(x, np.float32).astype(ml_dtypes.bfloat16).astype(np.float64), axis, -1)
    blocks = v.reshape(v.shape[:-1] + (-1, 32))
    amax = np.abs(blocks).max(-1, keepdims=True)
    byte = np.maximum(np.where(amax > 0, np.frexp(amax)[1] - 1 + 127, 0) - down, 1)
    scale = np.exp2(byte - 127.0)
    codes = (blocks / scale).astype(np.float32).astype(dtype).astype(np.float64)
    return np.moveaxis((codes * scale).reshape(v.shape), -1, axis)


WIDE = False


def mx_kscale(k):
    if not WIDE:
        return np.ones(k)
    levels = np.array([30, -30])
    if k % 512:
        return np.exp2(np.random.permutation(np.resize(levels, k // 32))).repeat(32)
    a = np.empty((k // 512, 16))
    for p in range(k // 512):
        a[p, :8] = np.random.permutation(np.resize(levels, 8))
        for g in range(8):
            far = levels[np.abs(levels - a[p, g]) >= 10]
            a[p, g + 8] = far[np.random.randint(len(far))]
    return np.exp2(a.ravel()).repeat(32)


BF16 = ml_dtypes.bfloat16


def bf(x):
    return np.asarray(x, np.float32).astype(BF16)


def f64(x):
    return np.asarray(x).astype(np.float64)


B, T, HID, H, D, QB = 1, 1024, 1536, 12, 128, 512
LN_EPS = 1e-5


def layer_norm(u):
    mu = u.mean(-1, keepdims=True)
    var = ((u - mu) ** 2).mean(-1, keepdims=True)
    return (u - mu) * (1.0 / np.sqrt(var + LN_EPS))


def feature_map(u, gamma, beta):
    return layer_norm(u * gamma + beta)


def setup_inputs():
    s = mx_kscale(HID)
    return {"hidden_states": bf(np.random.standard_normal((B, T, HID)) * s),
            "Wq": bf(np.random.standard_normal((H * D, HID)) / np.sqrt(HID) / s),
            "Wk": bf(np.random.standard_normal((H * D, HID)) / np.sqrt(HID) / s),
            "gamma": bf(1.0 + 0.1 * np.random.standard_normal(D)),
            "beta": bf(0.1 * np.random.standard_normal(D))}


def reference(hidden_states, Wq, Wk, gamma, beta):
    g, b = f64(gamma), f64(beta)
    xq = mxq(f64(hidden_states), 2, "e5m2")
    q = (xq @ mxq(f64(Wq), 1, "e4m3").T).reshape(B, T, H, D)
    k = (xq @ mxq(f64(Wk), 1, "e4m3").T).reshape(B, T, H, D)
    q_feat = feature_map(q, g, b) * (D ** -0.5)
    k_feat = feature_map(k, g, b)
    return q_feat, k_feat

@@ -1,0 +1,249 @@
+from contextlib import ExitStack
+
+import concourse.mybir as mybir
+from concourse.masks import make_identity
+
+T, HID, H, D = 1024, 1536, 12, 128
+LN_EPS = 1e-5
+FLOPS = 2 * 2 * T * HID * H * D
+
+F32 = mybir.dt.float32
+BF16 = mybir.dt.bfloat16
+U32 = mybir.dt.uint32
+U8 = mybir.dt.uint8
+E5M2X4 = mybir.dt.float8_e5m2_x4
+E4M3X4 = mybir.dt.float8_e4m3fn_x4
+ALU = mybir.AluOpType
+ACT = mybir.ActivationFunctionType
+
+P = 128
+PACK = 4
+K_PASS = P * PACK
+PASSES = HID // K_PASS
+WORDS = K_PASS // 2
+N_TILE = 512
+HEADS = N_TILE // D
+ROW_TILES = N_TILE // P
+TOKEN_TILES = T // P
+CHUNKS = 2 * H * D // N_TILE
+TILES = CHUNKS * TOKEN_TILES
+
+
+def tile_rebasedlinearattention_pa_kernel(tc, hidden_states, Wq, Wk, gamma, beta, out_0, out_1):
+    nc = tc.nc
+    x = hidden_states.rearrange("b t k -> (b t) k")
+    outs = [o.rearrange("b t h d -> (b t) (h d)") for o in (out_0, out_1)]
+    per_weight = CHUNKS // 2
+
+    with ExitStack() as ctx:
+        keep = ctx.enter_context(tc.tile_pool(name="keep", bufs=1))
+        work = ctx.enter_context(tc.tile_pool(name="work", bufs=2))
+        psum = ctx.enter_context(tc.psum_pool(name="psum", bufs=4))
+        ctx.enter_context(tc.manual_schedule())
+
+        ident = keep.tile([P, P], F32)
+        make_identity(nc, ident[:])
+
+        x_words, w_words = {}, {}
+        x_stage, w_stage = {}, {}
+        x_codes, x_scales, w_codes, w_scales = {}, {}, {}, {}
+        acc, scaled, affine, stats, rstd, shift = {}, {}, {}, {}, {}, {}
+
+        def w_rows(j):
+            w = (Wq, Wk)[j // per_weight]
+            r0 = (j % per_weight) * N_TILE
+            return w[r0 : r0 + N_TILE, :].rearrange("(t p) k -> p t k", p=P)
+
+        def load_x(i):
+            raw = keep.tile([P, HID], BF16, name="x_raw%d" % i)
+            nc.sync.dma_start(out=raw[:], in_=x[i * P : (i + 1) * P, :])
+            x_words[i] = raw[:].bitcast(F32)
+
+        def load_w_pass(j, g):
+            raw = keep.tile([P, ROW_TILES, K_PASS], BF16, name="w_first%d" % g)
+            nc.sync.dma_start(out=raw[:], in_=w_rows(j)[:, :, g * K_PASS : (g + 1) * K_PASS])
+            w_words[j, g] = raw[:].bitcast(F32)
+
+        def load_w(j):
+            raw = work.tile([P, ROW_TILES, HID], BF16, name="w_raw", bufs=3)
+            nc.sync.dma_start(out=raw[:], in_=w_rows(j))
+            for g in range(PASSES):
+                w_words[j, g] = raw[:].bitcast(F32)[:, :, g * WORDS : (g + 1) * WORDS]
+
+        def turn(sources, stage_words):
+            bank = psum.tile([P, 4, P], F32, name="turned")
+            for a, words in enumerate(sources):
+                for u in range(2):
+                    nc.tensor.transpose(bank[:, 2 * a + u, :], words[:, u:WORDS:2], ident[:])
+            n = len(sources)
+            nc.scalar.copy(
+                out=stage_words.rearrange("p (a r u) -> p a r u", a=n, u=2),
+                in_=bank[:, : 2 * n, :].rearrange("p (a u) r -> p a r u", u=2),
+            )
+
+        def turn_x(i):
+            stage = work.tile([P, HID], BF16, name="x_stage", bufs=3, align_bytes=64)
+            x_stage[i] = stage
+            words = stage[:].bitcast(F32)
+            src = [x_words[i][:, g * WORDS : (g + 1) * WORDS] for g in range(PASSES)]
+            turn(src[:2], words[:, : 2 * WORDS])
+            turn(src[2:], words[:, 2 * WORDS :])
+
+        def turn_w(j, g):
+            stage = work.tile([P, N_TILE * PACK], BF16, name="w_stage", bufs=3, align_bytes=64)
+            w_stage[j, g] = stage
+            words = stage[:].bitcast(F32)
+            for t in range(0, ROW_TILES, 2):
+                turn([w_words[j, g][:, t, :], w_words[j, g][:, t + 1, :]], words[:, t * WORDS : (t + 2) * WORDS])
+
+        def quantize_x(i):
+            codes = keep.tile([P, PASSES * P], U32, name="x_codes%d" % i, align_bytes=64)
+            scales = keep.tile([P, PASSES * P], U8, name="x_scales%d" % i, align_bytes=64)
+            x_codes[i], x_scales[i] = codes, scales
+            for c0, c1 in ((0, 2 * P), (2 * P, 3 * P)):
+                nc.vector.quantize_mx(
+                    out=codes[:, c0:c1].bitcast(E5M2X4),
+                    scales=scales[:, c0:c1],
+                    in_=x_stage[i][:, PACK * c0 : PACK * c1],
+                )
+
+        def quantize_w(j, g):
+            codes = keep.tile([P, N_TILE], U32, name="w_codes%d_%d" % (j, g), align_bytes=64)
+            scales = keep.tile([P, N_TILE], U8, name="w_scales%d_%d" % (j, g), align_bytes=64)
+            w_codes[j, g], w_scales[j, g] = codes, scales
+            nc.vector.quantize_mx(out=codes[:].bitcast(E4M3X4), scales=scales[:], in_=w_stage[j, g][:])
+
+        def multiply(n, g):
+            j, i = divmod(n, TOKEN_TILES)
+            if g == 0:
+                acc[n] = psum.tile([P, N_TILE], F32, name="acc")
+            cols = slice(g * P, (g + 1) * P)
+            nc.tensor.matmul_mx(
+                out=acc[n][:],
+                lhsT=x_codes[i][:, cols].bitcast(E5M2X4),
+                lhsT_scale=x_scales[i][:, cols],
+                rhs=w_codes[j, g][:].bitcast(E4M3X4),
+                rhs_scale=w_scales[j, g][:],
+                start=(g == 0),
+                stop=(g == PASSES - 1),
+            )
+
+        def scale_by_gamma(n):
+            scaled[n] = work.tile([P, N_TILE], F32, name="scaled", bufs=3)
+            nc.vector.tensor_tensor(out=scaled[n][:], in0=acc[n][:], in1=gamma_wide[:], op=ALU.mult)
+
+        def add_beta(n):
+            affine[n] = work.tile([P, N_TILE], F32, name="affine", bufs=7)
+            nc.gpsimd.tensor_tensor(out=affine[n][:], in0=scaled[n][:], in1=beta_wide[:], op=ALU.add)
+
+        def head_stats(n):
+            if n % 2 == 0:
+                stats[n // 2] = work.tile([P, 2 * HEADS, 3], F32, name="stats", bufs=3)
+            st = stats[n // 2]
+            for h in range(0, HEADS, 2):
+                slot = (n % 2) * HEADS + h
+                nc.vector.bn_stats(
+                    out=st[:, slot : slot + 2, :].rearrange("p e s -> p (e s)"),
+                    in_=affine[n][:, h * D : (h + 2) * D].rearrange("p (e d) -> p d e", e=2),
+                )
+
+        def inverse_std(m):
+            is_q = (2 * m) // TOKEN_TILES < per_weight
+            rstd[m] = work.tile([P, 2 * HEADS], F32, name="rstd", bufs=3)
+            nc.scalar.activation(
+                out=rstd[m][:],
+                in_=stats[m][:, :, 2],
+                func=ACT.Abs_reciprocal_sqrt,
+                scale=1.0 if is_q else 1.0 / D,
+                bias=LN_EPS * D if is_q else LN_EPS,
+            )
+
+        def mean_shift(m):
+            shift[m] = work.tile([P, 2 * HEADS], F32, name="shift", bufs=3)
+            nc.vector.scalar_tensor_tensor(
+                out=shift[m][:], in0=stats[m][:, :, 1], scalar=-1.0, in1=rstd[m][:], op0=ALU.mult, op1=ALU.mult
+            )
+
+        def normalise_and_store(n):
+            j, i = divmod(n, TOKEN_TILES)
+            feat = work.tile([P, N_TILE], F32, name="feat", bufs=8)
+            for h in range(HEADS):
+                slot = (n % 2) * HEADS + h
+                nc.scalar.activation(
+                    out=feat[:, h * D : (h + 1) * D],
+                    in_=affine[n][:, h * D : (h + 1) * D],
+                    func=ACT.Identity,
+                    scale=rstd[n // 2][:, slot : slot + 1],
+                    bias=shift[n // 2][:, slot : slot + 1],
+                )
+            c0 = (j % per_weight) * N_TILE
+            nc.sync.dma_start(out=outs[j // per_weight][i * P : (i + 1) * P, c0 : c0 + N_TILE], in_=feat[:])
+
+        load_x(0)
+        load_w_pass(0, 0)
+        load_x(1)
+        load_w_pass(0, 1)
+        load_w_pass(0, 2)
+        rows = keep.tile([P, 2, D], BF16, name="rows")
+        nc.sync.dma_start(out=rows[:, 0, :], in_=gamma.partition_broadcast(P))
+        nc.sync.dma_start(out=rows[:, 1, :], in_=beta.partition_broadcast(P))
+        load_x(2)
+        load_x(3)
+        load_w(1)
+        for i in range(4, TOKEN_TILES):
+            load_x(i)
+        load_w(2)
+
+        turn_x(0)
+        turn_w(0, 0)
+        quantize_x(0)
+        turn_x(1)
+        quantize_w(0, 0)
+        turn_w(0, 1)
+        quantize_x(1)
+        multiply(0, 0)
+        multiply(1, 0)
+        quantize_w(0, 1)
+        turn_w(0, 2)
+        multiply(0, 1)
+        multiply(1, 1)
+        gamma_wide = keep.tile([P, N_TILE], F32, name="gamma_wide")
+        beta_wide = keep.tile([P, N_TILE], F32, name="beta_wide")
+        for h in range(HEADS):
+            nc.vector.tensor_copy(out=gamma_wide[:, h * D : (h + 1) * D], in_=rows[:, 0, :])
+            nc.vector.tensor_copy(out=beta_wide[:, h * D : (h + 1) * D], in_=rows[:, 1, :])
+        quantize_w(0, 2)
+        turn_x(2)
+        multiply(0, 2)
+        multiply(1, 2)
+        quantize_x(2)
+
+        to_quantize = []
+        for n in range(TILES + 6):
+            j, i = divmod(n, TOKEN_TILES)
+            if n < TILES:
+                scale_by_gamma(n)
+            if n % 2 == 0 and 4 <= n < TILES + 4:
+                inverse_std((n - 4) // 2)
+            for step in to_quantize:
+                step[0](*step[1])
+            to_quantize = []
+            if n % 2 == 0 and 4 <= n < TILES + 4:
+                mean_shift((n - 4) // 2)
+            if n < TILES:
+                add_beta(n)
+            if n + 3 < TOKEN_TILES:
+                turn_x(n + 3)
+                to_quantize.append((quantize_x, (n + 3,)))
+            if j + 1 < CHUNKS and i in (0, 2, 4):
+                turn_w(j + 1, i // 2)
+                to_quantize.append((quantize_w, (j + 1, i // 2)))
+            if n + 2 < TILES:
+                for g in range(PASSES):
+                    multiply(n + 2, g)
+            if 2 <= n < TILES + 2:
+                head_stats(n - 2)
+            if 4 <= n < TILES + 4:
+                normalise_and_store(n - 4)
+            if i == 6 and j + 3 < CHUNKS:
+                load_w(j + 3)

@@ -27,6 +27,15 @@ ROW_TILES = N_TILE // P
 TOKEN_TILES = T // P
 CHUNKS = 2 * H * D // N_TILE
 TILES = CHUNKS * TOKEN_TILES
+BATCH = 2
+TAIL = 4
+TAIL_HEADS = (0, 2, 2)
+STAT_BUFS = 5
+SPREAD = (3, 1, 1, 1, 1, 1)
+EARLY = (0, 0, 1, 2, 3, 5, 7, 9, 11, 13)
+TURNS = (-1, 1, 3)
+LOCK = 4
+EXTRA_V = (47,)
 
 
 def tile_rebasedlinearattention_pa_kernel(tc, hidden_states, Wq, Wk, gamma, beta, out_0, out_1):
@@ -38,16 +47,18 @@ def tile_rebasedlinearattention_pa_kernel(tc, hidden_states, Wq, Wk, gamma, beta
     with ExitStack() as ctx:
         keep = ctx.enter_context(tc.tile_pool(name="keep", bufs=1))
         work = ctx.enter_context(tc.tile_pool(name="work", bufs=2))
-        psum = ctx.enter_context(tc.psum_pool(name="psum", bufs=4))
+        psum = ctx.enter_context(tc.psum_pool(name="psum", bufs=1))
         ctx.enter_context(tc.manual_schedule())
 
         ident = keep.tile([P, P], F32)
         make_identity(nc, ident[:])
 
-        x_words, w_words = {}, {}
-        x_stage, w_stage = {}, {}
-        x_codes, x_scales, w_codes, w_scales = {}, {}, {}, {}
-        acc, scaled, affine, stats, rstd, shift = {}, {}, {}, {}, {}, {}
+        raw_words, stage, codes, scales = {}, {}, {}, {}
+        acc, scaled, affine, stats, shift = {}, {}, {}, {}, {}
+        half_tiles = TOKEN_TILES // 2
+        order = [(i, j) for j in range(2) for i in range(half_tiles)]
+        order += [(i, j) for i in range(half_tiles, TOKEN_TILES) for j in range(2)]
+        order += [(i, j) for j in range(2, CHUNKS) for i in range(TOKEN_TILES)]
 
         def w_rows(j):
             w = (Wq, Wk)[j // per_weight]
@@ -57,21 +68,31 @@ def tile_rebasedlinearattention_pa_kernel(tc, hidden_states, Wq, Wk, gamma, beta
         def load_x(i):
             raw = keep.tile([P, HID], BF16, name="x_raw%d" % i)
             nc.sync.dma_start(out=raw[:], in_=x[i * P : (i + 1) * P, :])
-            x_words[i] = raw[:].bitcast(F32)
+            for g in range(PASSES):
+                raw_words["x", (i, g)] = raw[:].bitcast(F32)[:, g * WORDS : (g + 1) * WORDS]
 
         def load_w_pass(j, g):
             raw = keep.tile([P, ROW_TILES, K_PASS], BF16, name="w_first%d" % g)
             nc.sync.dma_start(out=raw[:], in_=w_rows(j)[:, :, g * K_PASS : (g + 1) * K_PASS])
-            w_words[j, g] = raw[:].bitcast(F32)
+            for t in range(ROW_TILES):
+                raw_words["w", (j, g, t)] = raw[:].bitcast(F32)[:, t, :]
 
         def load_w(j):
             raw = work.tile([P, ROW_TILES, HID], BF16, name="w_raw", bufs=3)
             nc.sync.dma_start(out=raw[:], in_=w_rows(j))
             for g in range(PASSES):
-                w_words[j, g] = raw[:].bitcast(F32)[:, :, g * WORDS : (g + 1) * WORDS]
+                for t in range(ROW_TILES):
+                    raw_words["w", (j, g, t)] = raw[:].bitcast(F32)[:, t, g * WORDS : (g + 1) * WORDS]
+
+        def w_unit(j, *gs):
+            return ("w", tuple((j, g, t) for g in gs for t in range(ROW_TILES)))
+
+        x_parts = [(i, g) for i in range(1, TOKEN_TILES) for g in range(PASSES)]
+        x_first = [("x", ((0, 0), (0, 1))), ("x", ((0, 2), x_parts[0]))]
+        x_units = [("x", tuple(x_parts[a : a + 4])) for a in range(1, len(x_parts), 4)]
 
         def turn(sources, stage_words):
-            bank = psum.tile([P, 4, P], F32, name="turned")
+            bank = psum.tile([P, 4, P], F32, name="turned", bufs=3)
             for a, words in enumerate(sources):
                 for u in range(2):
                     nc.tensor.transpose(bank[:, 2 * a + u, :], words[:, u:WORDS:2], ident[:])
@@ -81,49 +102,38 @@ def tile_rebasedlinearattention_pa_kernel(tc, hidden_states, Wq, Wk, gamma, beta
                 in_=bank[:, : 2 * n, :].rearrange("p (a u) r -> p a r u", u=2),
             )
 
-        def turn_x(i):
-            stage = work.tile([P, HID], BF16, name="x_stage", bufs=3, align_bytes=64)
-            x_stage[i] = stage
-            words = stage[:].bitcast(F32)
-            src = [x_words[i][:, g * WORDS : (g + 1) * WORDS] for g in range(PASSES)]
-            turn(src[:2], words[:, : 2 * WORDS])
-            turn(src[2:], words[:, 2 * WORDS :])
+        def turn_unit(unit, half):
+            name, parts = unit
+            if half == 0:
+                stage[unit] = work.tile([P, len(parts) * K_PASS], BF16, name="stage%d" % len(parts), bufs=3, align_bytes=64)
+            words = stage[unit][:].bitcast(F32)
+            for a in range(4 * half, min(4 * half + 4, len(parts)), 2):
+                both = parts[a : a + 2]
+                turn([raw_words[name, part] for part in both], words[:, a * WORDS : (a + len(both)) * WORDS])
 
-        def turn_w(j, g):
-            stage = work.tile([P, N_TILE * PACK], BF16, name="w_stage", bufs=3, align_bytes=64)
-            w_stage[j, g] = stage
-            words = stage[:].bitcast(F32)
-            for t in range(0, ROW_TILES, 2):
-                turn([w_words[j, g][:, t, :], w_words[j, g][:, t + 1, :]], words[:, t * WORDS : (t + 2) * WORDS])
-
-        def quantize_x(i):
-            codes = keep.tile([P, PASSES * P], U32, name="x_codes%d" % i, align_bytes=64)
-            scales = keep.tile([P, PASSES * P], U8, name="x_scales%d" % i, align_bytes=64)
-            x_codes[i], x_scales[i] = codes, scales
-            for c0, c1 in ((0, 2 * P), (2 * P, 3 * P)):
-                nc.vector.quantize_mx(
-                    out=codes[:, c0:c1].bitcast(E5M2X4),
-                    scales=scales[:, c0:c1],
-                    in_=x_stage[i][:, PACK * c0 : PACK * c1],
-                )
-
-        def quantize_w(j, g):
-            codes = keep.tile([P, N_TILE], U32, name="w_codes%d_%d" % (j, g), align_bytes=64)
-            scales = keep.tile([P, N_TILE], U8, name="w_scales%d_%d" % (j, g), align_bytes=64)
-            w_codes[j, g], w_scales[j, g] = codes, scales
-            nc.vector.quantize_mx(out=codes[:].bitcast(E4M3X4), scales=scales[:], in_=w_stage[j, g][:])
+        def quantize_unit(unit):
+            name, parts = unit
+            label = "%s%d_%d" % (name, parts[0][0], parts[0][1])
+            packed = keep.tile([P, len(parts) * P], U32, name="codes_" + label, align_bytes=64)
+            plane = keep.tile([P, len(parts) * P], U8, name="scales_" + label, align_bytes=64)
+            fmt = E5M2X4 if name == "x" else E4M3X4
+            nc.vector.quantize_mx(out=packed[:].bitcast(fmt), scales=plane[:], in_=stage[unit][:])
+            width = 1 if name == "x" else ROW_TILES
+            for a in range(0, len(parts), width):
+                key = (name,) + parts[a][:2]
+                codes[key] = packed[:, a * P : (a + width) * P]
+                scales[key] = plane[:, a * P : (a + width) * P]
 
         def multiply(n, g):
-            j, i = divmod(n, TOKEN_TILES)
+            i, j = order[n]
             if g == 0:
-                acc[n] = psum.tile([P, N_TILE], F32, name="acc")
-            cols = slice(g * P, (g + 1) * P)
+                acc[n] = psum.tile([P, N_TILE], F32, name="acc", bufs=4)
             nc.tensor.matmul_mx(
                 out=acc[n][:],
-                lhsT=x_codes[i][:, cols].bitcast(E5M2X4),
-                lhsT_scale=x_scales[i][:, cols],
-                rhs=w_codes[j, g][:].bitcast(E4M3X4),
-                rhs_scale=w_scales[j, g][:],
+                lhsT=codes["x", i, g].bitcast(E5M2X4),
+                lhsT_scale=scales["x", i, g],
+                rhs=codes["w", j, g].bitcast(E4M3X4),
+                rhs_scale=scales["w", j, g],
                 start=(g == 0),
                 stop=(g == PASSES - 1),
             )
@@ -132,118 +142,186 @@ def tile_rebasedlinearattention_pa_kernel(tc, hidden_states, Wq, Wk, gamma, beta
             scaled[n] = work.tile([P, N_TILE], F32, name="scaled", bufs=3)
             nc.vector.tensor_tensor(out=scaled[n][:], in0=acc[n][:], in1=gamma_wide[:], op=ALU.mult)
 
-        def add_beta(n):
-            affine[n] = work.tile([P, N_TILE], F32, name="affine", bufs=7)
-            nc.gpsimd.tensor_tensor(out=affine[n][:], in0=scaled[n][:], in1=beta_wide[:], op=ALU.add)
+        def add_beta(n, on_vector):
+            affine[n] = work.tile([P, N_TILE], F32, name="affine", bufs=10)
+            if on_vector:
+                nc.vector.tensor_tensor(out=affine[n][:], in0=scaled[n][:], in1=beta_bank[:], op=ALU.add)
+            else:
+                nc.gpsimd.tensor_tensor(out=affine[n][:], in0=scaled[n][:], in1=beta_wide[:], op=ALU.add)
 
-        def head_stats(n):
-            if n % 2 == 0:
-                stats[n // 2] = work.tile([P, 2 * HEADS, 3], F32, name="stats", bufs=3)
-            st = stats[n // 2]
+        def head_stats(n, batch):
+            if n == batch[0]:
+                stats[batch] = stat_tiles[len(stats) % STAT_BUFS]
             for h in range(0, HEADS, 2):
-                slot = (n % 2) * HEADS + h
+                slot = (n - batch[0]) * HEADS + h
                 nc.vector.bn_stats(
-                    out=st[:, slot : slot + 2, :].rearrange("p e s -> p (e s)"),
+                    out=stats[batch][:, slot : slot + 2, 1:4],
                     in_=affine[n][:, h * D : (h + 2) * D].rearrange("p (e d) -> p d e", e=2),
                 )
 
-        def inverse_std(m):
-            is_q = (2 * m) // TOKEN_TILES < per_weight
-            rstd[m] = work.tile([P, 2 * HEADS], F32, name="rstd", bufs=3)
+        def inverse_std(batch):
+            is_q = batch[0] < TILES // 2
+            slots = slice(0, len(batch) * HEADS)
             nc.scalar.activation(
-                out=rstd[m][:],
-                in_=stats[m][:, :, 2],
+                out=stats[batch][:, slots, 1],
+                in_=stats[batch][:, slots, 3],
                 func=ACT.Abs_reciprocal_sqrt,
                 scale=1.0 if is_q else 1.0 / D,
                 bias=LN_EPS * D if is_q else LN_EPS,
             )
 
-        def mean_shift(m):
-            shift[m] = work.tile([P, 2 * HEADS], F32, name="shift", bufs=3)
-            nc.vector.scalar_tensor_tensor(
-                out=shift[m][:], in0=stats[m][:, :, 1], scalar=-1.0, in1=rstd[m][:], op0=ALU.mult, op1=ALU.mult
-            )
+        def mean_shift(batch):
+            shift[batch] = work.tile([P, BATCH * HEADS], F32, name="shift", bufs=3)
+            slots = slice(0, len(batch) * HEADS)
+            nc.vector.tensor_reduce(out=shift[batch][:, slots], in_=stats[batch][:, slots, 0:3], axis=mybir.AxisListType.X, op=ALU.mult)
 
-        def normalise_and_store(n):
-            j, i = divmod(n, TOKEN_TILES)
+        def normalise_and_store(n, batch, vector_heads=0):
+            i, j = order[n]
             feat = work.tile([P, N_TILE], F32, name="feat", bufs=8)
             for h in range(HEADS):
-                slot = (n % 2) * HEADS + h
+                slot = (n - batch[0]) * HEADS + h
+                if h >= HEADS - vector_heads:
+                    nc.vector.tensor_scalar(
+                        out=feat[:, h * D : (h + 1) * D],
+                        in0=affine[n][:, h * D : (h + 1) * D],
+                        scalar1=stats[batch][:, slot, 1:2],
+                        scalar2=shift[batch][:, slot : slot + 1],
+                        op0=ALU.mult,
+                        op1=ALU.add,
+                    )
+                    continue
                 nc.scalar.activation(
                     out=feat[:, h * D : (h + 1) * D],
                     in_=affine[n][:, h * D : (h + 1) * D],
                     func=ACT.Identity,
-                    scale=rstd[n // 2][:, slot : slot + 1],
-                    bias=shift[n // 2][:, slot : slot + 1],
+                    scale=stats[batch][:, slot, 1:2],
+                    bias=shift[batch][:, slot : slot + 1],
                 )
             c0 = (j % per_weight) * N_TILE
             nc.sync.dma_start(out=outs[j // per_weight][i * P : (i + 1) * P, c0 : c0 + N_TILE], in_=feat[:])
 
+        rows_in = keep.tile([P, 2, D], BF16, name="rows_in")
+        rows = keep.tile([P, 2, D], F32, name="rows")
+        ones = keep.tile([P, P], F32, name="ones")
+        nc.vector.memset(rows_in[:], 0.0)
+        nc.vector.memset(ones[:], 1.0)
+        nc.sync.dma_start(out=rows_in[0:1, 0, :], in_=gamma.unsqueeze(0))
+        nc.sync.dma_start(out=rows_in[0:1, 1, :], in_=beta.unsqueeze(0))
+        nc.vector.tensor_copy(out=rows[:], in_=rows_in[:])
+        stat_tiles = []
+        for b in range(STAT_BUFS):
+            st = keep.tile([P, BATCH * HEADS, 4], F32, name="stats%d" % b)
+            nc.vector.memset(st[:, :, 0:1], -1.0)
+            stat_tiles.append(st)
+
+        gamma_bank = psum.tile([P, N_TILE], F32, name="acc", bufs=4)
+        beta_bank = psum.tile([P, N_TILE], F32, name="beta_bank")
+        spreads = [(which, h) for which in range(2) for h in range(HEADS)]
+
+        def spread(count):
+            for which, h in spreads[:count]:
+                bank = (gamma_bank, beta_bank)[which]
+                nc.tensor.matmul(out=bank[:, h * D : (h + 1) * D], lhsT=ones[:], rhs=rows[:, which, :], start=True, stop=True)
+            spreads[:] = spreads[count:]
+
+        gamma_wide = keep.tile([P, N_TILE], F32, name="gamma_wide")
+        beta_wide = keep.tile([P, N_TILE], F32, name="beta_wide")
+
         load_x(0)
         load_w_pass(0, 0)
-        load_x(1)
         load_w_pass(0, 1)
+        load_x(1)
         load_w_pass(0, 2)
-        rows = keep.tile([P, 2, D], BF16, name="rows")
-        nc.sync.dma_start(out=rows[:, 0, :], in_=gamma.partition_broadcast(P))
-        nc.sync.dma_start(out=rows[:, 1, :], in_=beta.partition_broadcast(P))
         load_x(2)
         load_x(3)
         load_w(1)
-        for i in range(4, TOKEN_TILES):
+        for i in range(half_tiles, TOKEN_TILES):
             load_x(i)
         load_w(2)
 
-        turn_x(0)
-        turn_w(0, 0)
-        quantize_x(0)
-        turn_x(1)
-        quantize_w(0, 0)
-        turn_w(0, 1)
-        quantize_x(1)
+        spread(SPREAD[0])
+        turn_unit(x_first[0], 0)
+        spread(SPREAD[1])
+        turn_unit(w_unit(0, 0), 0)
+        quantize_unit(x_first[0])
+        spread(SPREAD[2])
+        turn_unit(w_unit(0, 1), 0)
+        quantize_unit(w_unit(0, 0))
+        nc.vector.tensor_copy(out=gamma_wide[:], in_=gamma_bank[:])
+        spread(SPREAD[3])
+        turn_unit(x_first[1], 0)
+        quantize_unit(w_unit(0, 1))
         multiply(0, 0)
-        multiply(1, 0)
-        quantize_w(0, 1)
-        turn_w(0, 2)
+        spread(SPREAD[4])
+        turn_unit(w_unit(0, 2), 0)
+        quantize_unit(x_first[1])
         multiply(0, 1)
-        multiply(1, 1)
-        gamma_wide = keep.tile([P, N_TILE], F32, name="gamma_wide")
-        beta_wide = keep.tile([P, N_TILE], F32, name="beta_wide")
-        for h in range(HEADS):
-            nc.vector.tensor_copy(out=gamma_wide[:, h * D : (h + 1) * D], in_=rows[:, 0, :])
-            nc.vector.tensor_copy(out=beta_wide[:, h * D : (h + 1) * D], in_=rows[:, 1, :])
-        quantize_w(0, 2)
-        turn_x(2)
+        spread(SPREAD[5])
+        turn_unit(x_units[0], 0)
+        quantize_unit(w_unit(0, 2))
         multiply(0, 2)
-        multiply(1, 2)
-        quantize_x(2)
+        nc.vector.tensor_copy(out=beta_wide[:], in_=beta_bank[:])
 
-        to_quantize = []
-        for n in range(TILES + 6):
-            j, i = divmod(n, TOKEN_TILES)
-            if n < TILES:
-                scale_by_gamma(n)
-            if n % 2 == 0 and 4 <= n < TILES + 4:
-                inverse_std((n - 4) // 2)
-            for step in to_quantize:
-                step[0](*step[1])
-            to_quantize = []
-            if n % 2 == 0 and 4 <= n < TILES + 4:
-                mean_shift((n - 4) // 2)
-            if n < TILES:
-                add_beta(n)
-            if n + 3 < TOKEN_TILES:
-                turn_x(n + 3)
-                to_quantize.append((quantize_x, (n + 3,)))
-            if j + 1 < CHUNKS and i in (0, 2, 4):
-                turn_w(j + 1, i // 2)
-                to_quantize.append((quantize_w, (j + 1, i // 2)))
-            if n + 2 < TILES:
+        before, after, turns = {}, {0: [x_units[0]]}, {}
+        early = [x_units[1]] + [w_unit(1, g) for g in range(PASSES)] + x_units[2:] + [w_unit(2, g) for g in range(PASSES)]
+        for unit, when in zip(early, EARLY):
+            turns.setdefault(when, []).append((unit, 0))
+            after.setdefault(when + 1, []).append(unit)
+        on_vector = set(EXTRA_V)
+        for j in range(3, CHUNKS):
+            base = (j - 1) * TOKEN_TILES
+            lone, pair = w_unit(j, 0), w_unit(j, 1, 2)
+            lock = base + LOCK
+            turns.setdefault(base + TURNS[0], []).append((lone, 0))
+            turns.setdefault(base + TURNS[1], []).append((pair, 0))
+            turns.setdefault(base + TURNS[2], []).append((pair, 1))
+            before.setdefault(lock, []).append(lone)
+            after.setdefault(lock, []).append(pair)
+            on_vector.add(lock - 1)
+        products = {m - 1: [m] for m in range(1, TILES)}
+
+        batches = [tuple(range(n, n + BATCH)) for n in range(0, TILES - TAIL, BATCH)]
+        batches += [(n,) for n in range(TILES - TAIL, TILES)]
+        batch_of = {n: b for b in batches for n in b}
+        root_round = {b[-1] + (3 if len(b) > 1 else 2): b for b in batches if len(b) > 1}
+        singles = [b for b in batches if len(b) == 1]
+        waiting = []
+        for n in range(TILES):
+            for unit in before.get(n, []):
+                quantize_unit(unit)
+            scale_by_gamma(n)
+            for unit in after.get(n, []):
+                quantize_unit(unit)
+            if n not in on_vector:
+                add_beta(n, False)
+            for batch in (root_round.get(n - 1), (n - 3,)):
+                if batch in batches:
+                    mean_shift(batch)
+                    waiting += list(batch)
+            for unit, half in turns.get(n, []):
+                turn_unit(unit, half)
+            for m in products.get(n, []):
                 for g in range(PASSES):
-                    multiply(n + 2, g)
-            if 2 <= n < TILES + 2:
-                head_stats(n - 2)
-            if 4 <= n < TILES + 4:
-                normalise_and_store(n - 4)
-            if i == 6 and j + 3 < CHUNKS:
-                load_w(j + 3)
+                    multiply(m, g)
+            if n >= 2:
+                head_stats(n - 2, batch_of[n - 2])
+            if n in on_vector:
+                add_beta(n, True)
+            count = 2 if n >= TILES - TAIL else 1
+            for m in waiting[:count]:
+                normalise_and_store(m, batch_of[m])
+            waiting = waiting[count:]
+            for batch in (root_round.get(n), (n - 2,)):
+                if batch in batches:
+                    inverse_std(batch)
+            if n % TOKEN_TILES == 6 and n // TOKEN_TILES + 3 < CHUNKS:
+                load_w(n // TOKEN_TILES + 3)
+        for m in waiting:
+            normalise_and_store(m, batch_of[m])
+        for n in range(TILES - 3, TILES):
+            if n + 1 < TILES:
+                head_stats(n + 1, (n + 1,))
+            mean_shift((n,))
+            if n + 1 < TILES:
+                inverse_std((n + 1,))
+            normalise_and_store(n, (n,), TAIL_HEADS[n - TILES])

from contextlib import ExitStack

import concourse.mybir as mybir
from concourse.masks import make_identity

T, HID, H, D = 1024, 1536, 12, 128
LN_EPS = 1e-5
FLOPS = 2 * 2 * T * HID * H * D

F32 = mybir.dt.float32
BF16 = mybir.dt.bfloat16
U32 = mybir.dt.uint32
U8 = mybir.dt.uint8
E5M2X4 = mybir.dt.float8_e5m2_x4
E4M3X4 = mybir.dt.float8_e4m3fn_x4
ALU = mybir.AluOpType
ACT = mybir.ActivationFunctionType

P = 128
PACK = 4
K_PASS = P * PACK
PASSES = HID // K_PASS
WORDS = K_PASS // 2
N_TILE = 512
HEADS = N_TILE // D
ROW_TILES = N_TILE // P
TOKEN_TILES = T // P
CHUNKS = 2 * H * D // N_TILE
TILES = CHUNKS * TOKEN_TILES
BATCH = 2
TAIL = 4
TAIL_HEADS = (0, 2, 2)
STAT_BUFS = 5
SPREAD = (3, 1, 1, 1, 1, 1)
EARLY = (0, 0, 1, 2, 3, 5, 7, 9, 11, 13)
TURNS = (-1, 1, 3)
LOCK = 4
EXTRA_V = (47,)


def tile_rebasedlinearattention_pa_kernel(tc, hidden_states, Wq, Wk, gamma, beta, out_0, out_1):
    nc = tc.nc
    x = hidden_states.rearrange("b t k -> (b t) k")
    outs = [o.rearrange("b t h d -> (b t) (h d)") for o in (out_0, out_1)]
    per_weight = CHUNKS // 2

    with ExitStack() as ctx:
        keep = ctx.enter_context(tc.tile_pool(name="keep", bufs=1))
        work = ctx.enter_context(tc.tile_pool(name="work", bufs=2))
        psum = ctx.enter_context(tc.psum_pool(name="psum", bufs=1))
        ctx.enter_context(tc.manual_schedule())

        ident = keep.tile([P, P], F32)
        make_identity(nc, ident[:])

        raw_words, stage, codes, scales = {}, {}, {}, {}
        acc, scaled, affine, stats, shift = {}, {}, {}, {}, {}
        half_tiles = TOKEN_TILES // 2
        order = [(i, j) for j in range(2) for i in range(half_tiles)]
        order += [(i, j) for i in range(half_tiles, TOKEN_TILES) for j in range(2)]
        order += [(i, j) for j in range(2, CHUNKS) for i in range(TOKEN_TILES)]

        def w_rows(j):
            w = (Wq, Wk)[j // per_weight]
            r0 = (j % per_weight) * N_TILE
            return w[r0 : r0 + N_TILE, :].rearrange("(t p) k -> p t k", p=P)

        def load_x(i):
            raw = keep.tile([P, HID], BF16, name="x_raw%d" % i)
            nc.sync.dma_start(out=raw[:], in_=x[i * P : (i + 1) * P, :])
            for g in range(PASSES):
                raw_words["x", (i, g)] = raw[:].bitcast(F32)[:, g * WORDS : (g + 1) * WORDS]

        def load_w_pass(j, g):
            raw = keep.tile([P, ROW_TILES, K_PASS], BF16, name="w_first%d" % g)
            nc.sync.dma_start(out=raw[:], in_=w_rows(j)[:, :, g * K_PASS : (g + 1) * K_PASS])
            for t in range(ROW_TILES):
                raw_words["w", (j, g, t)] = raw[:].bitcast(F32)[:, t, :]

        def load_w(j):
            raw = work.tile([P, ROW_TILES, HID], BF16, name="w_raw", bufs=3)
            nc.sync.dma_start(out=raw[:], in_=w_rows(j))
            for g in range(PASSES):
                for t in range(ROW_TILES):
                    raw_words["w", (j, g, t)] = raw[:].bitcast(F32)[:, t, g * WORDS : (g + 1) * WORDS]

        def w_unit(j, *gs):
            return ("w", tuple((j, g, t) for g in gs for t in range(ROW_TILES)))

        x_parts = [(i, g) for i in range(1, TOKEN_TILES) for g in range(PASSES)]
        x_first = [("x", ((0, 0), (0, 1))), ("x", ((0, 2), x_parts[0]))]
        x_units = [("x", tuple(x_parts[a : a + 4])) for a in range(1, len(x_parts), 4)]

        def turn(sources, stage_words):
            bank = psum.tile([P, 4, P], F32, name="turned", bufs=3)
            for a, words in enumerate(sources):
                for u in range(2):
                    nc.tensor.transpose(bank[:, 2 * a + u, :], words[:, u:WORDS:2], ident[:])
            n = len(sources)
            nc.scalar.copy(
                out=stage_words.rearrange("p (a r u) -> p a r u", a=n, u=2),
                in_=bank[:, : 2 * n, :].rearrange("p (a u) r -> p a r u", u=2),
            )

        def turn_unit(unit, half):
            name, parts = unit
            if half == 0:
                stage[unit] = work.tile([P, len(parts) * K_PASS], BF16, name="stage%d" % len(parts), bufs=3, align_bytes=64)
            words = stage[unit][:].bitcast(F32)
            for a in range(4 * half, min(4 * half + 4, len(parts)), 2):
                both = parts[a : a + 2]
                turn([raw_words[name, part] for part in both], words[:, a * WORDS : (a + len(both)) * WORDS])

        def quantize_unit(unit):
            name, parts = unit
            label = "%s%d_%d" % (name, parts[0][0], parts[0][1])
            packed = keep.tile([P, len(parts) * P], U32, name="codes_" + label, align_bytes=64)
            plane = keep.tile([P, len(parts) * P], U8, name="scales_" + label, align_bytes=64)
            fmt = E5M2X4 if name == "x" else E4M3X4
            nc.vector.quantize_mx(out=packed[:].bitcast(fmt), scales=plane[:], in_=stage[unit][:])
            width = 1 if name == "x" else ROW_TILES
            for a in range(0, len(parts), width):
                key = (name,) + parts[a][:2]
                codes[key] = packed[:, a * P : (a + width) * P]
                scales[key] = plane[:, a * P : (a + width) * P]

        def multiply(n, g):
            i, j = order[n]
            if g == 0:
                acc[n] = psum.tile([P, N_TILE], F32, name="acc", bufs=4)
            nc.tensor.matmul_mx(
                out=acc[n][:],
                lhsT=codes["x", i, g].bitcast(E5M2X4),
                lhsT_scale=scales["x", i, g],
                rhs=codes["w", j, g].bitcast(E4M3X4),
                rhs_scale=scales["w", j, g],
                start=(g == 0),
                stop=(g == PASSES - 1),
            )

        def scale_by_gamma(n):
            scaled[n] = work.tile([P, N_TILE], F32, name="scaled", bufs=3)
            nc.vector.tensor_tensor(out=scaled[n][:], in0=acc[n][:], in1=gamma_wide[:], op=ALU.mult)

        def add_beta(n, on_vector):
            affine[n] = work.tile([P, N_TILE], F32, name="affine", bufs=10)
            if on_vector:
                nc.vector.tensor_tensor(out=affine[n][:], in0=scaled[n][:], in1=beta_bank[:], op=ALU.add)
            else:
                nc.gpsimd.tensor_tensor(out=affine[n][:], in0=scaled[n][:], in1=beta_wide[:], op=ALU.add)

        def head_stats(n, batch):
            if n == batch[0]:
                stats[batch] = stat_tiles[len(stats) % STAT_BUFS]
            for h in range(0, HEADS, 2):
                slot = (n - batch[0]) * HEADS + h
                nc.vector.bn_stats(
                    out=stats[batch][:, slot : slot + 2, 1:4],
                    in_=affine[n][:, h * D : (h + 2) * D].rearrange("p (e d) -> p d e", e=2),
                )

        def inverse_std(batch):
            is_q = batch[0] < TILES // 2
            slots = slice(0, len(batch) * HEADS)
            nc.scalar.activation(
                out=stats[batch][:, slots, 1],
                in_=stats[batch][:, slots, 3],
                func=ACT.Abs_reciprocal_sqrt,
                scale=1.0 if is_q else 1.0 / D,
                bias=LN_EPS * D if is_q else LN_EPS,
            )

        def mean_shift(batch):
            shift[batch] = work.tile([P, BATCH * HEADS], F32, name="shift", bufs=3)
            slots = slice(0, len(batch) * HEADS)
            nc.vector.tensor_reduce(out=shift[batch][:, slots], in_=stats[batch][:, slots, 0:3], axis=mybir.AxisListType.X, op=ALU.mult)

        def normalise_and_store(n, batch, vector_heads=0):
            i, j = order[n]
            feat = work.tile([P, N_TILE], F32, name="feat", bufs=8)
            for h in range(HEADS):
                slot = (n - batch[0]) * HEADS + h
                if h >= HEADS - vector_heads:
                    nc.vector.tensor_scalar(
                        out=feat[:, h * D : (h + 1) * D],
                        in0=affine[n][:, h * D : (h + 1) * D],
                        scalar1=stats[batch][:, slot, 1:2],
                        scalar2=shift[batch][:, slot : slot + 1],
                        op0=ALU.mult,
                        op1=ALU.add,
                    )
                    continue
                nc.scalar.activation(
                    out=feat[:, h * D : (h + 1) * D],
                    in_=affine[n][:, h * D : (h + 1) * D],
                    func=ACT.Identity,
                    scale=stats[batch][:, slot, 1:2],
                    bias=shift[batch][:, slot : slot + 1],
                )
            c0 = (j % per_weight) * N_TILE
            nc.sync.dma_start(out=outs[j // per_weight][i * P : (i + 1) * P, c0 : c0 + N_TILE], in_=feat[:])

        rows_in = keep.tile([P, 2, D], BF16, name="rows_in")
        rows = keep.tile([P, 2, D], F32, name="rows")
        ones = keep.tile([P, P], F32, name="ones")
        nc.vector.memset(rows_in[:], 0.0)
        nc.vector.memset(ones[:], 1.0)
        nc.sync.dma_start(out=rows_in[0:1, 0, :], in_=gamma.unsqueeze(0))
        nc.sync.dma_start(out=rows_in[0:1, 1, :], in_=beta.unsqueeze(0))
        nc.vector.tensor_copy(out=rows[:], in_=rows_in[:])
        stat_tiles = []
        for b in range(STAT_BUFS):
            st = keep.tile([P, BATCH * HEADS, 4], F32, name="stats%d" % b)
            nc.vector.memset(st[:, :, 0:1], -1.0)
            stat_tiles.append(st)

        gamma_bank = psum.tile([P, N_TILE], F32, name="acc", bufs=4)
        beta_bank = psum.tile([P, N_TILE], F32, name="beta_bank")
        spreads = [(which, h) for which in range(2) for h in range(HEADS)]

        def spread(count):
            for which, h in spreads[:count]:
                bank = (gamma_bank, beta_bank)[which]
                nc.tensor.matmul(out=bank[:, h * D : (h + 1) * D], lhsT=ones[:], rhs=rows[:, which, :], start=True, stop=True)
            spreads[:] = spreads[count:]

        gamma_wide = keep.tile([P, N_TILE], F32, name="gamma_wide")
        beta_wide = keep.tile([P, N_TILE], F32, name="beta_wide")

        load_x(0)
        load_w_pass(0, 0)
        load_w_pass(0, 1)
        load_x(1)
        load_w_pass(0, 2)
        load_x(2)
        load_x(3)
        load_w(1)
        for i in range(half_tiles, TOKEN_TILES):
            load_x(i)
        load_w(2)

        spread(SPREAD[0])
        turn_unit(x_first[0], 0)
        spread(SPREAD[1])
        turn_unit(w_unit(0, 0), 0)
        quantize_unit(x_first[0])
        spread(SPREAD[2])
        turn_unit(w_unit(0, 1), 0)
        quantize_unit(w_unit(0, 0))
        nc.vector.tensor_copy(out=gamma_wide[:], in_=gamma_bank[:])
        spread(SPREAD[3])
        turn_unit(x_first[1], 0)
        quantize_unit(w_unit(0, 1))
        multiply(0, 0)
        spread(SPREAD[4])
        turn_unit(w_unit(0, 2), 0)
        quantize_unit(x_first[1])
        multiply(0, 1)
        spread(SPREAD[5])
        turn_unit(x_units[0], 0)
        quantize_unit(w_unit(0, 2))
        multiply(0, 2)
        nc.vector.tensor_copy(out=beta_wide[:], in_=beta_bank[:])

        before, after, turns = {}, {0: [x_units[0]]}, {}
        early = [x_units[1]] + [w_unit(1, g) for g in range(PASSES)] + x_units[2:] + [w_unit(2, g) for g in range(PASSES)]
        for unit, when in zip(early, EARLY):
            turns.setdefault(when, []).append((unit, 0))
            after.setdefault(when + 1, []).append(unit)
        on_vector = set(EXTRA_V)
        for j in range(3, CHUNKS):
            base = (j - 1) * TOKEN_TILES
            lone, pair = w_unit(j, 0), w_unit(j, 1, 2)
            lock = base + LOCK
            turns.setdefault(base + TURNS[0], []).append((lone, 0))
            turns.setdefault(base + TURNS[1], []).append((pair, 0))
            turns.setdefault(base + TURNS[2], []).append((pair, 1))
            before.setdefault(lock, []).append(lone)
            after.setdefault(lock, []).append(pair)
            on_vector.add(lock - 1)
        products = {m - 1: [m] for m in range(1, TILES)}

        batches = [tuple(range(n, n + BATCH)) for n in range(0, TILES - TAIL, BATCH)]
        batches += [(n,) for n in range(TILES - TAIL, TILES)]
        batch_of = {n: b for b in batches for n in b}
        root_round = {b[-1] + (3 if len(b) > 1 else 2): b for b in batches if len(b) > 1}
        singles = [b for b in batches if len(b) == 1]
        waiting = []
        for n in range(TILES):
            for unit in before.get(n, []):
                quantize_unit(unit)
            scale_by_gamma(n)
            for unit in after.get(n, []):
                quantize_unit(unit)
            if n not in on_vector:
                add_beta(n, False)
            for batch in (root_round.get(n - 1), (n - 3,)):
                if batch in batches:
                    mean_shift(batch)
                    waiting += list(batch)
            for unit, half in turns.get(n, []):
                turn_unit(unit, half)
            for m in products.get(n, []):
                for g in range(PASSES):
                    multiply(m, g)
            if n >= 2:
                head_stats(n - 2, batch_of[n - 2])
            if n in on_vector:
                add_beta(n, True)
            count = 2 if n >= TILES - TAIL else 1
            for m in waiting[:count]:
                normalise_and_store(m, batch_of[m])
            waiting = waiting[count:]
            for batch in (root_round.get(n), (n - 2,)):
                if batch in batches:
                    inverse_std(batch)
            if n % TOKEN_TILES == 6 and n // TOKEN_TILES + 3 < CHUNKS:
                load_w(n // TOKEN_TILES + 3)
        for m in waiting:
            normalise_and_store(m, batch_of[m])
        for n in range(TILES - 3, TILES):
            if n + 1 < TILES:
                head_stats(n + 1, (n + 1,))
            mean_shift((n,))
            if n + 1 < TILES:
                inverse_std((n + 1,))
            normalise_and_store(n, (n,), TAIL_HEADS[n - TILES])
